import numpy as np
import ml_dtypes


def mxq(x, axis, fmt="e4m3"):
    dtype, down = {"e4m3": (ml_dtypes.float8_e4m3fn, 7), "e5m2": (ml_dtypes.float8_e5m2, 14)}[fmt]
    v = np.moveaxis(np.asarray(x, np.float32).astype(ml_dtypes.bfloat16).astype(np.float64), axis, -1)
    blocks = v.reshape(v.shape[:-1] + (-1, 32))
    amax = np.abs(blocks).max(-1, keepdims=True)
    byte = np.maximum(np.where(amax > 0, np.frexp(amax)[1] - 1 + 127, 0) - down, 1)
    scale = np.exp2(byte - 127.0)
    codes = (blocks / scale).astype(np.float32).astype(dtype).astype(np.float64)
    return np.moveaxis((codes * scale).reshape(v.shape), -1, axis)


WIDE = False


def mx_kscale(k):
    if not WIDE:
        return np.ones(k)
    levels = np.array([10, -10, 5, -5, 0])
    a = np.random.permutation(np.resize(levels, k // 512 * 4)).reshape(k // 512, 4)
    idx = np.arange(k)
    return np.exp2(a[idx // 512, idx % 128 // 32])


BF16 = ml_dtypes.bfloat16


def bf(x):
    return np.asarray(x, np.float32).astype(BF16)


def f64(x):
    return np.asarray(x).astype(np.float64)


B, L, LQ, DM, DH, W = 1, 4096, 1024, 1024, 128, 512
C = L // W


def chunk_banks(x):
    z = np.zeros_like(x[:, :1])
    prev = np.concatenate((z, x[:, :-1]), axis=1)
    nxt = np.concatenate((x[:, 1:], z), axis=1)
    return np.stack((prev, x, nxt), axis=1).sum(axis=2)


def setup_inputs():
    s = mx_kscale(DM)
    return {"kv": bf(np.random.standard_normal((B, L, DM)) * s),
            "Wkv": bf(np.random.standard_normal((DM, 2 * DH)) * 2.0 / np.sqrt(DM * C) / s[:, None])}


def reference(kv, Wkv):
    kvp = mxq(f64(kv), 2, "e4m3") @ mxq(f64(Wkv), 0, "e4m3")
    k, v = kvp[..., :DH], kvp[..., DH:]
    return chunk_banks(k.reshape(B, C, W, DH)), v

@@ -1,0 +1,217 @@
+from contextlib import ExitStack
+
+import concourse.mybir as mybir
+from concourse.masks import make_identity
+
+F32 = mybir.dt.float32
+BF16 = mybir.dt.bfloat16
+U32 = mybir.dt.uint32
+U8 = mybir.dt.uint8
+FP8X4 = mybir.dt.float8_e4m3fn_x4
+ADD = mybir.AluOpType.add
+
+P = 128
+L = 4096
+DM = 1024
+DH = 128
+CHUNK = 512
+CHUNKS = L // CHUNK
+
+FLOPS = 2 * L * DM * 2 * DH
+
+PACK = 4
+K_PASS = P * PACK
+PASSES = DM // K_PASS
+PAIRS = 2
+BLOCKS = PASSES * PAIRS
+
+ROWS = 2
+HALVES = CHUNK // (ROWS * P)
+UNITS = HALVES * CHUNKS
+UNIT_WORDS = ROWS * PASSES * P
+
+UNITS_PER_ROUND = 2
+ROUNDS = UNITS // UNITS_PER_ROUND
+ROUNDS_PER_HALF = ROUNDS // HALVES
+TRANSPOSE_BANKS = UNITS_PER_ROUND * ROWS
+
+VECTOR_BANK = 0
+
+ROUNDS_BUFFERED = 3
+
+FIRST, MIDDLE, LAST = 0, 1, 2
+
+
+def tile_localxlattention_pa_kernel(tc, kv, Wkv, out_0, out_1):
+    nc = tc.nc
+
+    kv_units = kv.rearrange(
+        "b (c h p j) k -> (b c) h p j k", c=CHUNKS, h=HALVES, p=P, j=ROWS
+    )
+    v_rounds = out_1.rearrange(
+        "b (q i h p j) d -> (b q) h p i j d",
+        q=ROUNDS_PER_HALF, i=UNITS_PER_ROUND, h=HALVES, p=P, j=ROWS,
+    )
+    k_ext_halves = out_0.rearrange("b s (h p j) d -> (b h) p s j d", h=HALVES, p=P, j=ROWS)
+
+    with ExitStack() as ctx:
+        ctx.enter_context(tc.manual_schedule())
+        consts = ctx.enter_context(tc.tile_pool(name="consts", bufs=1))
+        loads = ctx.enter_context(tc.tile_pool(name="loads", bufs=UNITS))
+        stage = ctx.enter_context(
+            tc.tile_pool(name="stage", bufs=ROUNDS_BUFFERED * UNITS_PER_ROUND)
+        )
+        results = ctx.enter_context(tc.tile_pool(name="results", bufs=ROUNDS))
+        xt_banks = ctx.enter_context(tc.psum_pool(name="xt_banks", bufs=TRANSPOSE_BANKS))
+        v_banks = ctx.enter_context(tc.psum_pool(name="v_banks", bufs=2))
+        k_banks = ctx.enter_context(tc.psum_pool(name="k_banks", bufs=ROWS))
+
+        identity = consts.tile([P, P], F32)
+        make_identity(nc, identity[:])
+
+        kv_tiles = []
+
+        def load_unit(n):
+            h, c = divmod(n, CHUNKS)
+            x_sb = loads.tile([P, ROWS * DM], BF16)
+            nc.sync.dma_start(
+                out=x_sb[:].rearrange("p (j k) -> p j k", j=ROWS), in_=kv_units[c, h]
+            )
+            kv_tiles.append(x_sb)
+
+        for n in range(UNITS_PER_ROUND):
+            load_unit(n)
+        w_raw = consts.tile([P, BLOCKS * 2 * 2 * DH], BF16)
+        nc.sync.dma_start(
+            out=w_raw[:].rearrange("p (s e n) -> p s e n", s=BLOCKS, e=2),
+            in_=Wkv.rearrange("(s p e) n -> p s e n", s=BLOCKS, p=P, e=2),
+        )
+        for n in range(UNITS_PER_ROUND, UNITS):
+            load_unit(n)
+
+        w_codes = consts.tile([P, PASSES * 2 * DH], U32, align_bytes=64)
+        w_scales = consts.tile([P, PASSES * 2 * DH], U8, align_bytes=64)
+
+        def quantise_weights():
+            w_grouped = consts.tile([P, PASSES * 2 * DH * PACK], BF16, align_bytes=64)
+            nc.vector.tensor_copy(
+                out=w_grouped[:].rearrange("p (g n t) -> p g n t", g=PASSES, t=PACK),
+                in_=w_raw[:].rearrange("p (g t n) -> p g n t", g=PASSES, t=PACK),
+            )
+            nc.vector.quantize_mx(
+                out=w_codes[:].bitcast(FP8X4), scales=w_scales[:], in_=w_grouped[:]
+            )
+
+        grouped_tiles = {}
+        code_tiles = {}
+
+        def transpose_round(r):
+            for i in range(UNITS_PER_ROUND):
+                n = r * UNITS_PER_ROUND + i
+                x_words = kv_tiles[n][:].bitcast(F32)
+                grouped = stage.tile([P, UNIT_WORDS * PACK], BF16, align_bytes=64)
+                grouped_words = grouped[:].bitcast(F32)
+                for j in range(ROWS):
+                    row = slice(j * BLOCKS * P, (j + 1) * BLOCKS * P)
+                    xt = xt_banks.tile([P, BLOCKS * P], F32)
+                    for s in range(BLOCKS):
+                        nc.tensor.transpose(
+                            out=xt[:, s * P : (s + 1) * P],
+                            in_=x_words[:, (j * BLOCKS + s) * P : (j * BLOCKS + s + 1) * P],
+                            identity=identity[:],
+                        )
+                    if i * ROWS + j == VECTOR_BANK:
+                        copy_out = nc.vector.tensor_copy
+                    else:
+                        copy_out = nc.scalar.copy
+                    copy_out(
+                        out=grouped_words[:, row].rearrange(
+                            "p (g r u) -> p g r u", g=PASSES, u=PAIRS
+                        ),
+                        in_=xt[:].rearrange("p (g u r) -> p g r u", g=PASSES, u=PAIRS),
+                    )
+                grouped_tiles[n] = grouped
+
+        def quantise_round(r):
+            for i in range(UNITS_PER_ROUND):
+                n = r * UNITS_PER_ROUND + i
+                codes = stage.tile([P, UNIT_WORDS], U32, align_bytes=64)
+                scales = stage.tile([P, UNIT_WORDS], U8, align_bytes=64)
+                nc.vector.quantize_mx(
+                    out=codes[:].bitcast(FP8X4), scales=scales[:], in_=grouped_tiles[n][:]
+                )
+                code_tiles[n] = (codes, scales)
+
+        k_groups = {}
+
+        def multiply_round(r):
+            h, q = divmod(r, ROUNDS_PER_HALF)
+            if q == 0:
+                for j in range(ROWS):
+                    k_ps = k_banks.tile([P, 3 * DH], F32)
+                    k_groups[(h, j)] = k_ps
+            v_ps = v_banks.tile([P, UNITS_PER_ROUND * ROWS * DH], F32)
+            for i in range(UNITS_PER_ROUND):
+                c = q * UNITS_PER_ROUND + i
+                codes, scales = code_tiles[r * UNITS_PER_ROUND + i]
+                if c == 0:
+                    place, opens, closes = FIRST, True, True
+                elif c == CHUNKS - 1:
+                    place, opens, closes = LAST, True, True
+                else:
+                    place, opens, closes = MIDDLE, c == 1, c == CHUNKS - 2
+                for j in range(ROWS):
+                    for g in range(PASSES):
+                        x_cols = slice((j * PASSES + g) * P, (j * PASSES + g + 1) * P)
+                        k_cols = slice(g * 2 * DH, g * 2 * DH + DH)
+                        v_cols = slice(g * 2 * DH + DH, (g + 1) * 2 * DH)
+                        nc.tensor.matmul_mx(
+                            out=k_groups[(h, j)][:, place * DH : (place + 1) * DH],
+                            lhsT=codes[:, x_cols].bitcast(FP8X4),
+                            lhsT_scale=scales[:, x_cols],
+                            rhs=w_codes[:, k_cols].bitcast(FP8X4),
+                            rhs_scale=w_scales[:, k_cols],
+                            start=(opens and g == 0),
+                            stop=(closes and g == PASSES - 1),
+                        )
+                        nc.tensor.matmul_mx(
+                            out=v_ps[:, (i * ROWS + j) * DH : (i * ROWS + j + 1) * DH],
+                            lhsT=codes[:, x_cols].bitcast(FP8X4),
+                            lhsT_scale=scales[:, x_cols],
+                            rhs=w_codes[:, v_cols].bitcast(FP8X4),
+                            rhs_scale=w_scales[:, v_cols],
+                            start=(g == 0),
+                            stop=(g == PASSES - 1),
+                        )
+            v_sb = results.tile([P, UNITS_PER_ROUND * ROWS * DH], F32)
+            nc.scalar.copy(out=v_sb[:], in_=v_ps[:])
+            nc.sync.dma_start(
+                out=v_rounds[q, h],
+                in_=v_sb[:].rearrange("p (i j d) -> p i j d", i=UNITS_PER_ROUND, j=ROWS),
+            )
+            if q == ROUNDS_PER_HALF - 1:
+                store_chunk_sums(h)
+
+        def store_chunk_sums(h):
+            k_ext_sb = results.tile([P, 3 * ROWS * DH], F32)
+            banks = k_ext_sb[:].rearrange("p (s j d) -> p s j d", s=3, j=ROWS)
+            for j in range(ROWS):
+                k_ps = k_groups[(h, j)]
+                first = k_ps[:, FIRST * DH : (FIRST + 1) * DH]
+                middle = k_ps[:, MIDDLE * DH : (MIDDLE + 1) * DH]
+                last = k_ps[:, LAST * DH : (LAST + 1) * DH]
+                middle_sb = results.tile([P, DH], F32)
+                nc.scalar.copy(out=middle_sb[:], in_=middle)
+                nc.vector.tensor_tensor(out=banks[:, 0, j, :], in0=first, in1=middle_sb[:], op=ADD)
+                nc.vector.tensor_tensor(out=banks[:, 2, j, :], in0=last, in1=middle_sb[:], op=ADD)
+                nc.vector.tensor_tensor(out=banks[:, 1, j, :], in0=last, in1=banks[:, 0, j, :], op=ADD)
+            nc.sync.dma_start(out=k_ext_halves[h], in_=banks)
+
+        transpose_round(0)
+        quantise_weights()
+        quantise_round(0)
+        for r in range(1, ROUNDS):
+            transpose_round(r)
+            multiply_round(r - 1)
+            quantise_round(r)
+        multiply_round(ROUNDS - 1)

@@ -55,7 +55,6 @@ def tile_localxlattention_pa_kernel(tc, kv, Wkv, out_0, out_1):
     k_ext_halves = out_0.rearrange("b s (h p j) d -> (b h) p s j d", h=HALVES, p=P, j=ROWS)
 
     with ExitStack() as ctx:
-        ctx.enter_context(tc.manual_schedule())
         consts = ctx.enter_context(tc.tile_pool(name="consts", bufs=1))
         loads = ctx.enter_context(tc.tile_pool(name="loads", bufs=UNITS))
         stage = ctx.enter_context(

@@ -35,8 +35,6 @@ ROUNDS = UNITS // UNITS_PER_ROUND
 ROUNDS_PER_HALF = ROUNDS // HALVES
 TRANSPOSE_BANKS = UNITS_PER_ROUND * ROWS
 
-VECTOR_BANK = 0
-
 ROUNDS_BUFFERED = 3
 
 FIRST, MIDDLE, LAST = 0, 1, 2
@@ -55,6 +53,7 @@ def tile_localxlattention_pa_kernel(tc, kv, Wkv, out_0, out_1):
     k_ext_halves = out_0.rearrange("b s (h p j) d -> (b h) p s j d", h=HALVES, p=P, j=ROWS)
 
     with ExitStack() as ctx:
+        ctx.enter_context(tc.manual_schedule())
         consts = ctx.enter_context(tc.tile_pool(name="consts", bufs=1))
         loads = ctx.enter_context(tc.tile_pool(name="loads", bufs=UNITS))
         stage = ctx.enter_context(
@@ -119,10 +118,7 @@ def tile_localxlattention_pa_kernel(tc, kv, Wkv, out_0, out_1):
                             in_=x_words[:, (j * BLOCKS + s) * P : (j * BLOCKS + s + 1) * P],
                             identity=identity[:],
                         )
-                    if i * ROWS + j == VECTOR_BANK:
-                        copy_out = nc.vector.tensor_copy
-                    else:
-                        copy_out = nc.scalar.copy
+                    copy_out = nc.vector.tensor_copy if j == 0 else nc.scalar.copy
                     copy_out(
                         out=grouped_words[:, row].rearrange(
                             "p (g r u) -> p g r u", g=PASSES, u=PAIRS
@@ -143,16 +139,31 @@ def tile_localxlattention_pa_kernel(tc, kv, Wkv, out_0, out_1):
 
         k_groups = {}
 
+        def multiply_row(out, n, j, w_first, opens, closes):
+            codes, scales = code_tiles[n]
+            for g in range(PASSES):
+                x_cols = slice((j * PASSES + g) * P, (j * PASSES + g + 1) * P)
+                w_cols = slice(g * 2 * DH + w_first, g * 2 * DH + w_first + DH)
+                nc.tensor.matmul_mx(
+                    out=out,
+                    lhsT=codes[:, x_cols].bitcast(FP8X4),
+                    lhsT_scale=scales[:, x_cols],
+                    rhs=w_codes[:, w_cols].bitcast(FP8X4),
+                    rhs_scale=w_scales[:, w_cols],
+                    start=(opens and g == 0),
+                    stop=(closes and g == PASSES - 1),
+                )
+
         def multiply_round(r):
             h, q = divmod(r, ROUNDS_PER_HALF)
+            half_done = q == ROUNDS_PER_HALF - 1
             if q == 0:
                 for j in range(ROWS):
                     k_ps = k_banks.tile([P, 3 * DH], F32)
                     k_groups[(h, j)] = k_ps
-            v_ps = v_banks.tile([P, UNITS_PER_ROUND * ROWS * DH], F32)
+
             for i in range(UNITS_PER_ROUND):
                 c = q * UNITS_PER_ROUND + i
-                codes, scales = code_tiles[r * UNITS_PER_ROUND + i]
                 if c == 0:
                     place, opens, closes = FIRST, True, True
                 elif c == CHUNKS - 1:
@@ -160,38 +171,33 @@ def tile_localxlattention_pa_kernel(tc, kv, Wkv, out_0, out_1):
                 else:
                     place, opens, closes = MIDDLE, c == 1, c == CHUNKS - 2
                 for j in range(ROWS):
-                    for g in range(PASSES):
-                        x_cols = slice((j * PASSES + g) * P, (j * PASSES + g + 1) * P)
-                        k_cols = slice(g * 2 * DH, g * 2 * DH + DH)
-                        v_cols = slice(g * 2 * DH + DH, (g + 1) * 2 * DH)
-                        nc.tensor.matmul_mx(
-                            out=k_groups[(h, j)][:, place * DH : (place + 1) * DH],
-                            lhsT=codes[:, x_cols].bitcast(FP8X4),
-                            lhsT_scale=scales[:, x_cols],
-                            rhs=w_codes[:, k_cols].bitcast(FP8X4),
-                            rhs_scale=w_scales[:, k_cols],
-                            start=(opens and g == 0),
-                            stop=(closes and g == PASSES - 1),
-                        )
-                        nc.tensor.matmul_mx(
-                            out=v_ps[:, (i * ROWS + j) * DH : (i * ROWS + j + 1) * DH],
-                            lhsT=codes[:, x_cols].bitcast(FP8X4),
-                            lhsT_scale=scales[:, x_cols],
-                            rhs=w_codes[:, v_cols].bitcast(FP8X4),
-                            rhs_scale=w_scales[:, v_cols],
-                            start=(g == 0),
-                            stop=(g == PASSES - 1),
-                        )
+                    multiply_row(
+                        k_groups[(h, j)][:, place * DH : (place + 1) * DH],
+                        r * UNITS_PER_ROUND + i, j, 0, opens, closes,
+                    )
+            if half_done:
+                k_ext_sb = add_chunk_sums(h)
+
+            v_ps = v_banks.tile([P, UNITS_PER_ROUND * ROWS * DH], F32)
+            for i in range(UNITS_PER_ROUND):
+                for j in range(ROWS):
+                    multiply_row(
+                        v_ps[:, (i * ROWS + j) * DH : (i * ROWS + j + 1) * DH],
+                        r * UNITS_PER_ROUND + i, j, DH, True, True,
+                    )
             v_sb = results.tile([P, UNITS_PER_ROUND * ROWS * DH], F32)
             nc.scalar.copy(out=v_sb[:], in_=v_ps[:])
             nc.sync.dma_start(
                 out=v_rounds[q, h],
                 in_=v_sb[:].rearrange("p (i j d) -> p i j d", i=UNITS_PER_ROUND, j=ROWS),
             )
-            if q == ROUNDS_PER_HALF - 1:
-                store_chunk_sums(h)
+            if half_done:
+                nc.sync.dma_start(
+                    out=k_ext_halves[h],
+                    in_=k_ext_sb[:].rearrange("p (s j d) -> p s j d", s=3, j=ROWS),
+                )
 
-        def store_chunk_sums(h):
+        def add_chunk_sums(h):
             k_ext_sb = results.tile([P, 3 * ROWS * DH], F32)
             banks = k_ext_sb[:].rearrange("p (s j d) -> p s j d", s=3, j=ROWS)
             for j in range(ROWS):
@@ -204,13 +210,13 @@ def tile_localxlattention_pa_kernel(tc, kv, Wkv, out_0, out_1):
                 nc.vector.tensor_tensor(out=banks[:, 0, j, :], in0=first, in1=middle_sb[:], op=ADD)
                 nc.vector.tensor_tensor(out=banks[:, 2, j, :], in0=last, in1=middle_sb[:], op=ADD)
                 nc.vector.tensor_tensor(out=banks[:, 1, j, :], in0=last, in1=banks[:, 0, j, :], op=ADD)
-            nc.sync.dma_start(out=k_ext_halves[h], in_=banks)
+            return k_ext_sb
 
         transpose_round(0)
         quantise_weights()
         quantise_round(0)
         for r in range(1, ROUNDS):
             transpose_round(r)
-            multiply_round(r - 1)
             quantise_round(r)
+            multiply_round(r - 1)
         multiply_round(ROUNDS - 1)

@@ -53,7 +53,6 @@ def tile_localxlattention_pa_kernel(tc, kv, Wkv, out_0, out_1):
     k_ext_halves = out_0.rearrange("b s (h p j) d -> (b h) p s j d", h=HALVES, p=P, j=ROWS)
 
     with ExitStack() as ctx:
-        ctx.enter_context(tc.manual_schedule())
         consts = ctx.enter_context(tc.tile_pool(name="consts", bufs=1))
         loads = ctx.enter_context(tc.tile_pool(name="loads", bufs=UNITS))
         stage = ctx.enter_context(

@@ -37,7 +37,8 @@ TRANSPOSE_BANKS = UNITS_PER_ROUND * ROWS
 
 ROUNDS_BUFFERED = 3
 
-FIRST, MIDDLE, LAST = 0, 1, 2
+CHUNK_ORDER = [0, CHUNKS - 1] + list(range(1, CHUNKS - 1))
+assert UNITS_PER_ROUND == 2
 
 
 def tile_localxlattention_pa_kernel(tc, kv, Wkv, out_0, out_1):
@@ -46,13 +47,13 @@ def tile_localxlattention_pa_kernel(tc, kv, Wkv, out_0, out_1):
     kv_units = kv.rearrange(
         "b (c h p j) k -> (b c) h p j k", c=CHUNKS, h=HALVES, p=P, j=ROWS
     )
-    v_rounds = out_1.rearrange(
-        "b (q i h p j) d -> (b q) h p i j d",
-        q=ROUNDS_PER_HALF, i=UNITS_PER_ROUND, h=HALVES, p=P, j=ROWS,
+    v_units = out_1.rearrange(
+        "b (c h p j) d -> (b c) h p j d", c=CHUNKS, h=HALVES, p=P, j=ROWS
     )
     k_ext_halves = out_0.rearrange("b s (h p j) d -> (b h) p s j d", h=HALVES, p=P, j=ROWS)
 
     with ExitStack() as ctx:
+        ctx.enter_context(tc.manual_schedule())
         consts = ctx.enter_context(tc.tile_pool(name="consts", bufs=1))
         loads = ctx.enter_context(tc.tile_pool(name="loads", bufs=UNITS))
         stage = ctx.enter_context(
@@ -60,8 +61,8 @@ def tile_localxlattention_pa_kernel(tc, kv, Wkv, out_0, out_1):
         )
         results = ctx.enter_context(tc.tile_pool(name="results", bufs=ROUNDS))
         xt_banks = ctx.enter_context(tc.psum_pool(name="xt_banks", bufs=TRANSPOSE_BANKS))
-        v_banks = ctx.enter_context(tc.psum_pool(name="v_banks", bufs=2))
-        k_banks = ctx.enter_context(tc.psum_pool(name="k_banks", bufs=ROWS))
+        closed_banks = ctx.enter_context(tc.psum_pool(name="closed_banks", bufs=2))
+        open_banks = ctx.enter_context(tc.psum_pool(name="open_banks", bufs=ROWS))
 
         identity = consts.tile([P, P], F32)
         make_identity(nc, identity[:])
@@ -69,10 +70,11 @@ def tile_localxlattention_pa_kernel(tc, kv, Wkv, out_0, out_1):
         kv_tiles = []
 
         def load_unit(n):
-            h, c = divmod(n, CHUNKS)
+            h, turn = divmod(n, CHUNKS)
             x_sb = loads.tile([P, ROWS * DM], BF16)
             nc.sync.dma_start(
-                out=x_sb[:].rearrange("p (j k) -> p j k", j=ROWS), in_=kv_units[c, h]
+                out=x_sb[:].rearrange("p (j k) -> p j k", j=ROWS),
+                in_=kv_units[CHUNK_ORDER[turn], h],
             )
             kv_tiles.append(x_sb)
 
@@ -136,8 +138,6 @@ def tile_localxlattention_pa_kernel(tc, kv, Wkv, out_0, out_1):
                 )
                 code_tiles[n] = (codes, scales)
 
-        k_groups = {}
-
         def multiply_row(out, n, j, w_first, opens, closes):
             codes, scales = code_tiles[n]
             for g in range(PASSES):
@@ -153,63 +153,67 @@ def tile_localxlattention_pa_kernel(tc, kv, Wkv, out_0, out_1):
                     stop=(closes and g == PASSES - 1),
                 )
 
+        def multiply_closed(r, w_first):
+            products = closed_banks.tile([P, UNITS_PER_ROUND * ROWS * DH], F32)
+            for i in range(UNITS_PER_ROUND):
+                for j in range(ROWS):
+                    multiply_row(
+                        products[:, (i * ROWS + j) * DH : (i * ROWS + j + 1) * DH],
+                        r * UNITS_PER_ROUND + i, j, w_first, True, True,
+                    )
+            return products
+
+        k_ext_tiles = {}
+        middle_sums = {}
+
         def multiply_round(r):
             h, q = divmod(r, ROUNDS_PER_HALF)
             half_done = q == ROUNDS_PER_HALF - 1
             if q == 0:
-                for j in range(ROWS):
-                    k_ps = k_banks.tile([P, 3 * DH], F32)
-                    k_groups[(h, j)] = k_ps
-
-            for i in range(UNITS_PER_ROUND):
-                c = q * UNITS_PER_ROUND + i
-                if c == 0:
-                    place, opens, closes = FIRST, True, True
-                elif c == CHUNKS - 1:
-                    place, opens, closes = LAST, True, True
-                else:
-                    place, opens, closes = MIDDLE, c == 1, c == CHUNKS - 2
-                for j in range(ROWS):
-                    multiply_row(
-                        k_groups[(h, j)][:, place * DH : (place + 1) * DH],
-                        r * UNITS_PER_ROUND + i, j, 0, opens, closes,
-                    )
+                edge_keys = multiply_closed(r, 0)
+                k_ext_sb = results.tile([P, 3 * ROWS * DH], F32)
+                k_ext_tiles[h] = k_ext_sb
+                banks = k_ext_sb[:].rearrange("p (s j d) -> p s j d", s=3, j=ROWS)
+                nc.scalar.copy(
+                    out=banks[:, 0:3:2, :, :],
+                    in_=edge_keys[:].rearrange("p (i j d) -> p i j d", i=UNITS_PER_ROUND, j=ROWS),
+                )
+                nc.vector.tensor_tensor(
+                    out=banks[:, 1, :, :], in0=banks[:, 0, :, :], in1=banks[:, 2, :, :], op=ADD
+                )
+            else:
+                if q == 1:
+                    for j in range(ROWS):
+                        middle_ps = open_banks.tile([P, DH], F32)
+                        middle_sums[(h, j)] = middle_ps
+                for i in range(UNITS_PER_ROUND):
+                    for j in range(ROWS):
+                        multiply_row(
+                            middle_sums[(h, j)][:], r * UNITS_PER_ROUND + i, j, 0,
+                            q == 1 and i == 0, half_done and i == UNITS_PER_ROUND - 1,
+                        )
             if half_done:
-                k_ext_sb = add_chunk_sums(h)
-
-            v_ps = v_banks.tile([P, UNITS_PER_ROUND * ROWS * DH], F32)
-            for i in range(UNITS_PER_ROUND):
+                banks = k_ext_tiles[h][:].rearrange("p (s j d) -> p s j d", s=3, j=ROWS)
                 for j in range(ROWS):
-                    multiply_row(
-                        v_ps[:, (i * ROWS + j) * DH : (i * ROWS + j + 1) * DH],
-                        r * UNITS_PER_ROUND + i, j, DH, True, True,
+                    nc.vector.tensor_tensor(
+                        out=banks[:, :, j, :],
+                        in0=middle_sums[(h, j)][:].unsqueeze(1).to_broadcast([P, 3, DH]),
+                        in1=banks[:, :, j, :],
+                        op=ADD,
                     )
+
+            v_ps = multiply_closed(r, DH)
             v_sb = results.tile([P, UNITS_PER_ROUND * ROWS * DH], F32)
             nc.scalar.copy(out=v_sb[:], in_=v_ps[:])
-            nc.sync.dma_start(
-                out=v_rounds[q, h],
-                in_=v_sb[:].rearrange("p (i j d) -> p i j d", i=UNITS_PER_ROUND, j=ROWS),
-            )
-            if half_done:
+            for i in range(UNITS_PER_ROUND):
                 nc.sync.dma_start(
-                    out=k_ext_halves[h],
-                    in_=k_ext_sb[:].rearrange("p (s j d) -> p s j d", s=3, j=ROWS),
+                    out=v_units[CHUNK_ORDER[q * UNITS_PER_ROUND + i], h],
+                    in_=v_sb[:, i * ROWS * DH : (i + 1) * ROWS * DH].rearrange(
+                        "p (j d) -> p j d", j=ROWS
+                    ),
                 )
-
-        def add_chunk_sums(h):
-            k_ext_sb = results.tile([P, 3 * ROWS * DH], F32)
-            banks = k_ext_sb[:].rearrange("p (s j d) -> p s j d", s=3, j=ROWS)
-            for j in range(ROWS):
-                k_ps = k_groups[(h, j)]
-                first = k_ps[:, FIRST * DH : (FIRST + 1) * DH]
-                middle = k_ps[:, MIDDLE * DH : (MIDDLE + 1) * DH]
-                last = k_ps[:, LAST * DH : (LAST + 1) * DH]
-                middle_sb = results.tile([P, DH], F32)
-                nc.scalar.copy(out=middle_sb[:], in_=middle)
-                nc.vector.tensor_tensor(out=banks[:, 0, j, :], in0=first, in1=middle_sb[:], op=ADD)
-                nc.vector.tensor_tensor(out=banks[:, 2, j, :], in0=last, in1=middle_sb[:], op=ADD)
-                nc.vector.tensor_tensor(out=banks[:, 1, j, :], in0=last, in1=banks[:, 0, j, :], op=ADD)
-            return k_ext_sb
+            if half_done:
+                nc.sync.dma_start(out=k_ext_halves[h], in_=banks)
 
         transpose_round(0)
         quantise_weights()

from contextlib import ExitStack

import concourse.mybir as mybir
from concourse.masks import make_identity

F32 = mybir.dt.float32
BF16 = mybir.dt.bfloat16
U32 = mybir.dt.uint32
U8 = mybir.dt.uint8
FP8X4 = mybir.dt.float8_e4m3fn_x4
ADD = mybir.AluOpType.add

P = 128
L = 4096
DM = 1024
DH = 128
CHUNK = 512
CHUNKS = L // CHUNK

FLOPS = 2 * L * DM * 2 * DH

PACK = 4
K_PASS = P * PACK
PASSES = DM // K_PASS
PAIRS = 2
BLOCKS = PASSES * PAIRS

ROWS = 2
HALVES = CHUNK // (ROWS * P)
UNITS = HALVES * CHUNKS
UNIT_WORDS = ROWS * PASSES * P

UNITS_PER_ROUND = 2
ROUNDS = UNITS // UNITS_PER_ROUND
ROUNDS_PER_HALF = ROUNDS // HALVES
TRANSPOSE_BANKS = UNITS_PER_ROUND * ROWS

ROUNDS_BUFFERED = 3

CHUNK_ORDER = [0, CHUNKS - 1] + list(range(1, CHUNKS - 1))
assert UNITS_PER_ROUND == 2


def tile_localxlattention_pa_kernel(tc, kv, Wkv, out_0, out_1):
    nc = tc.nc

    kv_units = kv.rearrange(
        "b (c h p j) k -> (b c) h p j k", c=CHUNKS, h=HALVES, p=P, j=ROWS
    )
    v_units = out_1.rearrange(
        "b (c h p j) d -> (b c) h p j d", c=CHUNKS, h=HALVES, p=P, j=ROWS
    )
    k_ext_halves = out_0.rearrange("b s (h p j) d -> (b h) p s j d", h=HALVES, p=P, j=ROWS)

    with ExitStack() as ctx:
        ctx.enter_context(tc.manual_schedule())
        consts = ctx.enter_context(tc.tile_pool(name="consts", bufs=1))
        loads = ctx.enter_context(tc.tile_pool(name="loads", bufs=UNITS))
        stage = ctx.enter_context(
            tc.tile_pool(name="stage", bufs=ROUNDS_BUFFERED * UNITS_PER_ROUND)
        )
        results = ctx.enter_context(tc.tile_pool(name="results", bufs=ROUNDS))
        xt_banks = ctx.enter_context(tc.psum_pool(name="xt_banks", bufs=TRANSPOSE_BANKS))
        closed_banks = ctx.enter_context(tc.psum_pool(name="closed_banks", bufs=2))
        open_banks = ctx.enter_context(tc.psum_pool(name="open_banks", bufs=ROWS))

        identity = consts.tile([P, P], F32)
        make_identity(nc, identity[:])

        kv_tiles = []

        def load_unit(n):
            h, turn = divmod(n, CHUNKS)
            x_sb = loads.tile([P, ROWS * DM], BF16)
            nc.sync.dma_start(
                out=x_sb[:].rearrange("p (j k) -> p j k", j=ROWS),
                in_=kv_units[CHUNK_ORDER[turn], h],
            )
            kv_tiles.append(x_sb)

        for n in range(UNITS_PER_ROUND):
            load_unit(n)
        w_raw = consts.tile([P, BLOCKS * 2 * 2 * DH], BF16)
        nc.sync.dma_start(
            out=w_raw[:].rearrange("p (s e n) -> p s e n", s=BLOCKS, e=2),
            in_=Wkv.rearrange("(s p e) n -> p s e n", s=BLOCKS, p=P, e=2),
        )
        for n in range(UNITS_PER_ROUND, UNITS):
            load_unit(n)

        w_codes = consts.tile([P, PASSES * 2 * DH], U32, align_bytes=64)
        w_scales = consts.tile([P, PASSES * 2 * DH], U8, align_bytes=64)

        def quantise_weights():
            w_grouped = consts.tile([P, PASSES * 2 * DH * PACK], BF16, align_bytes=64)
            nc.vector.tensor_copy(
                out=w_grouped[:].rearrange("p (g n t) -> p g n t", g=PASSES, t=PACK),
                in_=w_raw[:].rearrange("p (g t n) -> p g n t", g=PASSES, t=PACK),
            )
            nc.vector.quantize_mx(
                out=w_codes[:].bitcast(FP8X4), scales=w_scales[:], in_=w_grouped[:]
            )

        grouped_tiles = {}
        code_tiles = {}

        def transpose_round(r):
            for i in range(UNITS_PER_ROUND):
                n = r * UNITS_PER_ROUND + i
                x_words = kv_tiles[n][:].bitcast(F32)
                grouped = stage.tile([P, UNIT_WORDS * PACK], BF16, align_bytes=64)
                grouped_words = grouped[:].bitcast(F32)
                for j in range(ROWS):
                    row = slice(j * BLOCKS * P, (j + 1) * BLOCKS * P)
                    xt = xt_banks.tile([P, BLOCKS * P], F32)
                    for s in range(BLOCKS):
                        nc.tensor.transpose(
                            out=xt[:, s * P : (s + 1) * P],
                            in_=x_words[:, (j * BLOCKS + s) * P : (j * BLOCKS + s + 1) * P],
                            identity=identity[:],
                        )
                    copy_out = nc.vector.tensor_copy if j == 0 else nc.scalar.copy
                    copy_out(
                        out=grouped_words[:, row].rearrange(
                            "p (g r u) -> p g r u", g=PASSES, u=PAIRS
                        ),
                        in_=xt[:].rearrange("p (g u r) -> p g r u", g=PASSES, u=PAIRS),
                    )
                grouped_tiles[n] = grouped

        def quantise_round(r):
            for i in range(UNITS_PER_ROUND):
                n = r * UNITS_PER_ROUND + i
                codes = stage.tile([P, UNIT_WORDS], U32, align_bytes=64)
                scales = stage.tile([P, UNIT_WORDS], U8, align_bytes=64)
                nc.vector.quantize_mx(
                    out=codes[:].bitcast(FP8X4), scales=scales[:], in_=grouped_tiles[n][:]
                )
                code_tiles[n] = (codes, scales)

        def multiply_row(out, n, j, w_first, opens, closes):
            codes, scales = code_tiles[n]
            for g in range(PASSES):
                x_cols = slice((j * PASSES + g) * P, (j * PASSES + g + 1) * P)
                w_cols = slice(g * 2 * DH + w_first, g * 2 * DH + w_first + DH)
                nc.tensor.matmul_mx(
                    out=out,
                    lhsT=codes[:, x_cols].bitcast(FP8X4),
                    lhsT_scale=scales[:, x_cols],
                    rhs=w_codes[:, w_cols].bitcast(FP8X4),
                    rhs_scale=w_scales[:, w_cols],
                    start=(opens and g == 0),
                    stop=(closes and g == PASSES - 1),
                )

        def multiply_closed(r, w_first):
            products = closed_banks.tile([P, UNITS_PER_ROUND * ROWS * DH], F32)
            for i in range(UNITS_PER_ROUND):
                for j in range(ROWS):
                    multiply_row(
                        products[:, (i * ROWS + j) * DH : (i * ROWS + j + 1) * DH],
                        r * UNITS_PER_ROUND + i, j, w_first, True, True,
                    )
            return products

        k_ext_tiles = {}
        middle_sums = {}

        def multiply_round(r):
            h, q = divmod(r, ROUNDS_PER_HALF)
            half_done = q == ROUNDS_PER_HALF - 1
            if q == 0:
                edge_keys = multiply_closed(r, 0)
                k_ext_sb = results.tile([P, 3 * ROWS * DH], F32)
                k_ext_tiles[h] = k_ext_sb
                banks = k_ext_sb[:].rearrange("p (s j d) -> p s j d", s=3, j=ROWS)
                nc.scalar.copy(
                    out=banks[:, 0:3:2, :, :],
                    in_=edge_keys[:].rearrange("p (i j d) -> p i j d", i=UNITS_PER_ROUND, j=ROWS),
                )
                nc.vector.tensor_tensor(
                    out=banks[:, 1, :, :], in0=banks[:, 0, :, :], in1=banks[:, 2, :, :], op=ADD
                )
            else:
                if q == 1:
                    for j in range(ROWS):
                        middle_ps = open_banks.tile([P, DH], F32)
                        middle_sums[(h, j)] = middle_ps
                for i in range(UNITS_PER_ROUND):
                    for j in range(ROWS):
                        multiply_row(
                            middle_sums[(h, j)][:], r * UNITS_PER_ROUND + i, j, 0,
                            q == 1 and i == 0, half_done and i == UNITS_PER_ROUND - 1,
                        )
            if half_done:
                banks = k_ext_tiles[h][:].rearrange("p (s j d) -> p s j d", s=3, j=ROWS)
                for j in range(ROWS):
                    nc.vector.tensor_tensor(
                        out=banks[:, :, j, :],
                        in0=middle_sums[(h, j)][:].unsqueeze(1).to_broadcast([P, 3, DH]),
                        in1=banks[:, :, j, :],
                        op=ADD,
                    )

            v_ps = multiply_closed(r, DH)
            v_sb = results.tile([P, UNITS_PER_ROUND * ROWS * DH], F32)
            nc.scalar.copy(out=v_sb[:], in_=v_ps[:])
            for i in range(UNITS_PER_ROUND):
                nc.sync.dma_start(
                    out=v_units[CHUNK_ORDER[q * UNITS_PER_ROUND + i], h],
                    in_=v_sb[:, i * ROWS * DH : (i + 1) * ROWS * DH].rearrange(
                        "p (j d) -> p j d", j=ROWS
                    ),
                )
            if half_done:
                nc.sync.dma_start(out=k_ext_halves[h], in_=banks)

        transpose_round(0)
        quantise_weights()
        quantise_round(0)
        for r in range(1, ROUNDS):
            transpose_round(r)
            quantise_round(r)
            multiply_round(r - 1)
        multiply_round(ROUNDS - 1)
